import numpy as np
import ml_dtypes


def mxq(x, axis, fmt="e4m3"):
    dtype, down = {"e4m3": (ml_dtypes.float8_e4m3fn, 7), "e5m2": (ml_dtypes.float8_e5m2, 14)}[fmt]
    v = np.moveaxis(np.asarray(x, np.float32).astype(ml_dtypes.bfloat16).astype(np.float64), axis, -1)
    blocks = v.reshape(v.shape[:-1] + (-1, 32))
    amax = np.abs(blocks).max(-1, keepdims=True)
    byte = np.maximum(np.where(amax > 0, np.frexp(amax)[1] - 1 + 127, 0) - down, 1)
    scale = np.exp2(byte - 127.0)
    codes = (blocks / scale).astype(np.float32).astype(dtype).astype(np.float64)
    return np.moveaxis((codes * scale).reshape(v.shape), -1, axis)


WIDE = False


def mx_kscale(k):
    if not WIDE:
        return np.ones(k)
    levels = np.array([10, -10, 5, -5, 0])
    a = np.random.permutation(np.resize(levels, k // 512 * 4)).reshape(k // 512, 4)
    idx = np.arange(k)
    return np.exp2(a[idx // 512, idx % 128 // 32])


BF16 = ml_dtypes.bfloat16


def bf(x):
    return np.asarray(x, np.float32).astype(BF16)


def f64(x):
    return np.asarray(x).astype(np.float64)


E2M1 = np.array([0.0, 0.5, 1.0, 1.5, 2.0, 3.0, 4.0, 6.0, -0.0, -0.5, -1.0, -1.5, -2.0, -3.0, -4.0, -6.0])


def pack_weight(w, fmt):
    k, n = w.shape
    w = f64(bf(w)).reshape(k // 32, 32, n)
    amax = np.abs(w).max(1)
    if fmt == "e4m3":
        byte = np.frexp(amax)[1] - 1 + 127 - 7
    else:
        mant, ex = np.frexp(amax / 6.0)
        byte = np.where(mant > 0.5, ex, ex - 1) + 127
    byte = np.clip(np.where(amax > 0, byte, 1), 1, 254)
    scaled = (w * np.exp2(127.0 - byte)[:, None, :]).reshape(k, n).astype(np.float32)
    by_word = np.ascontiguousarray(scaled.reshape(k // 512, 128, 4, n).transpose(0, 1, 3, 2))
    if fmt == "e4m3":
        words = by_word.astype(ml_dtypes.float8_e4m3fn).view(np.uint8)
    else:
        c = by_word.astype(ml_dtypes.float4_e2m1fn).view(np.uint8) & 0xF
        words = c[..., 0::2] | (c[..., 1::2] << 4)
    return np.ascontiguousarray(words), np.ascontiguousarray(byte.astype(np.uint8).reshape(k // 512, 16, n))


def unpack_weight(words, scales, fmt):
    g, p, n, _ = words.shape
    if fmt == "e4m3":
        vals = np.ascontiguousarray(words).view(ml_dtypes.float8_e4m3fn).astype(np.float64)
    else:
        nib = np.empty((g, p, n, 4), np.uint8)
        nib[..., 0::2] = words & 0xF
        nib[..., 1::2] = words >> 4
        vals = E2M1[nib]
    vals = vals * np.repeat(np.exp2(scales.astype(np.float64) - 127.0), 8, axis=1)[..., None]
    return vals.transpose(0, 1, 3, 2).reshape(g * 512, n)

def pack4(w):
    words, scales = pack_weight(w, "e2m1")
    return words.reshape(words.shape[0], 128, -1), scales


def unpack4(words, scales):
    return unpack_weight(words.reshape(words.shape[0], 128, -1, 2), scales, "e2m1")


B, T, C, H, NOPE, ROPE, VD, LORA = 1, 128, 8192, 16, 128, 128, 128, 512
QK = NOPE + ROPE
HALF = ROPE // 2


def make_freq_cis():
    inv = 1.0 / (10000.0 ** (np.arange(0, ROPE, 2) / ROPE))
    ang = np.outer(np.arange(T), inv)
    return np.stack([np.cos(ang), np.sin(ang)], -1)


def apply_rope(v, fc):
    vr = v.reshape(B, T, H, HALF, 2)
    f = fc.reshape(1, T, 1, HALF, 2)
    real = vr[..., 0] * f[..., 0] - vr[..., 1] * f[..., 1]
    imag = vr[..., 1] * f[..., 0] + vr[..., 0] * f[..., 1]
    return np.stack([real, imag], -1).reshape(B, T, H, ROPE)


def setup_inputs():
    s = mx_kscale(C)
    x = bf(np.random.standard_normal((B, T, C)) * s)
    freq_cis = bf(make_freq_cis())
    words, scales = pack4(np.random.standard_normal((C, H * QK)) * 2.0 / np.sqrt(C) / s[:, None])
    return {"x": x,
            "freq_cis": freq_cis,
            "Wq_words": words,
            "Wq_scales": scales}


def reference(x, freq_cis, Wq_words, Wq_scales):
    q = (mxq(f64(x), 2, "e4m3") @ unpack4(Wq_words, Wq_scales)).reshape(B, T, H, QK)
    q_nope, q_rope = q[..., :NOPE], q[..., NOPE:]
    q_rope = apply_rope(q_rope, f64(freq_cis))
    return np.concatenate([q_nope, q_rope], -1)

@@ -1,0 +1,174 @@
+from contextlib import ExitStack
+
+import concourse.mybir as mybir
+from concourse.masks import make_identity
+
+BF16 = mybir.dt.bfloat16
+F32 = mybir.dt.float32
+I32 = mybir.dt.int32
+U8 = mybir.dt.uint8
+U32 = mybir.dt.uint32
+FP8X4 = mybir.dt.float8_e4m3fn_x4
+FP4X4 = mybir.dt.float4_e2m1fn_x4
+
+P = 128
+K = 8192
+N = 4096
+K_GROUP = 512
+GROUPS = K // K_GROUP
+BANK = 512
+BANKS = N // BANK
+HEAD = 256
+NOPE = 128
+ROPE = 128
+PAIRS = ROPE // 2
+HEADS_PER_BANK = BANK // HEAD
+
+FINISH_GROUPS = 4
+BODY_GROUPS = GROUPS - FINISH_GROUPS
+
+SCALE_GROUPS_PER_DMA = 2
+QUANT_GROUPS = 4
+W_BUFS = 8
+PIECE_BUFS = 4
+
+FLOPS = 2 * P * K * N
+
+
+def tile_multiheadlatentattention_pb_k_kernel(tc, x, freq_cis, Wq_words, Wq_scales, out):
+    nc = tc.nc
+    x_rows = x.rearrange("b t k -> (b t) k")
+    out_rows = out.rearrange("b t h d -> (b t) (h d)")
+    w_words_dram = Wq_words.bitcast(I32)
+    w_scales_dram = Wq_scales.bitcast(I32)
+
+    with ExitStack() as ctx:
+        keep = ctx.enter_context(tc.tile_pool(name="keep", bufs=1))
+        w_pool = ctx.enter_context(tc.tile_pool(name="w_pool", bufs=W_BUFS))
+        piece_pool = ctx.enter_context(tc.tile_pool(name="piece_pool", bufs=PIECE_BUFS))
+        work = ctx.enter_context(tc.tile_pool(name="work", bufs=2))
+        psum = ctx.enter_context(tc.psum_pool(name="psum", bufs=BANKS))
+        ctx.enter_context(tc.manual_schedule())
+
+        x_sb = keep.tile([P, K], BF16, align_bytes=64)
+        nc.sync.dma_start(out=x_sb[:], in_=x_rows)
+        angles = keep.tile([P, PAIRS, 2], BF16)
+        nc.scalar.dma_start(out=angles[:], in_=freq_cis)
+
+        identity = keep.tile([P, P], F32)
+        make_identity(nc, identity[:])
+
+        w_planes = keep.tile([P, GROUPS, N], U8, align_bytes=64)
+        for g0 in range(0, GROUPS, SCALE_GROUPS_PER_DMA):
+            nc.vector.memset(w_planes[:, g0 : g0 + SCALE_GROUPS_PER_DMA, :].bitcast(I32), 0)
+
+        for g0 in range(0, GROUPS, SCALE_GROUPS_PER_DMA):
+            g_sel = slice(g0, g0 + SCALE_GROUPS_PER_DMA)
+            for q in range(8):
+                partition = 32 * (q // 4) + q % 4
+                nc.sync.dma_start(
+                    out=w_planes[partition:P:64, g_sel, :].bitcast(I32),
+                    in_=w_scales_dram[g_sel, q:16:8, :].rearrange("g j n -> j g n"),
+                )
+
+        x_pairs = x_sb[:].bitcast(F32)
+        grouped = keep.tile([P, GROUPS, P, 4], BF16, align_bytes=64)
+        x_codes = keep.tile([P, GROUPS, P], U32, align_bytes=64)
+        x_planes = keep.tile([P, GROUPS, P], U8, align_bytes=64)
+        for g0 in range(0, GROUPS, 2):
+            flipped = psum.tile([P, 2, 2, P], F32, tag="bank")
+            for i in range(2):
+                first = (K_GROUP // 2) * (g0 + i)
+                for u in range(2):
+                    nc.tensor.transpose(
+                        flipped[:, i, u, :],
+                        x_pairs[:, first + u : first + K_GROUP // 2 : 2],
+                        identity[:],
+                    )
+            nc.scalar.copy(
+                out=grouped[:, g0 : g0 + 2]
+                .rearrange("p g n t -> p g (n t)")
+                .bitcast(F32)
+                .rearrange("p g (n u) -> p g n u", u=2),
+                in_=flipped[:].rearrange("p g u n -> p g n u"),
+            )
+
+        cos_twice = keep.tile([P, PAIRS, 2], F32)
+        nc.vector.tensor_copy(out=cos_twice[:], in_=angles[:, :, 0:1].to_broadcast([P, PAIRS, 2]))
+        sin_plus = keep.tile([P, PAIRS], F32)
+        nc.vector.tensor_copy(out=sin_plus[:], in_=angles[:, :, 1])
+        sin_minus = keep.tile([P, PAIRS], F32)
+        nc.vector.tensor_scalar_mul(out=sin_minus[:], in0=angles[:, :, 1], scalar1=-1.0)
+
+        for g0 in range(0, GROUPS, QUANT_GROUPS):
+            g_sel = slice(g0, g0 + QUANT_GROUPS)
+            nc.vector.quantize_mx(
+                out=x_codes[:, g_sel, :].rearrange("p g n -> p (g n)").bitcast(FP8X4),
+                scales=x_planes[:, g_sel, :].rearrange("p g n -> p (g n)"),
+                in_=grouped[:, g_sel].rearrange("p g n t -> p (g n t)"),
+            )
+
+        def one_pass(acc, g, bank, w_codes):
+            nc.tensor.matmul_mx(
+                out=acc[:],
+                lhsT=x_codes[:, g, :].bitcast(FP8X4),
+                lhsT_scale=x_planes[:, g, :],
+                rhs=w_codes.bitcast(FP4X4),
+                rhs_scale=w_planes[:, g, bank * BANK : (bank + 1) * BANK],
+                start=(g == 0),
+                stop=(g == GROUPS - 1),
+            )
+
+        accs = [psum.tile([P, BANK], F32, tag="bank", name="acc%d" % bank) for bank in range(BANKS)]
+        for g in range(BODY_GROUPS):
+            w_group = w_pool.tile([P, 2 * N], U8, align_bytes=64)
+            nc.sync.dma_start(out=w_group[:].bitcast(I32), in_=w_words_dram[g])
+            for bank in range(BANKS):
+                one_pass(accs[bank], g, bank, w_group[:, bank * 2 * BANK : (bank + 1) * 2 * BANK])
+
+        result = keep.tile([P, BANKS, HEADS_PER_BANK, HEAD], F32)
+        for bank in range(BANKS):
+            piece = piece_pool.tile([P, FINISH_GROUPS, 2 * BANK], U8, align_bytes=64)
+            nc.sync.dma_start(
+                out=piece[:].bitcast(I32),
+                in_=w_words_dram[BODY_GROUPS:GROUPS, :, bank * BANK // 2 : (bank + 1) * BANK // 2].rearrange(
+                    "g p n -> p g n"
+                ),
+            )
+            for i in range(FINISH_GROUPS):
+                one_pass(accs[bank], BODY_GROUPS + i, bank, piece[:, i, :])
+
+            heads = accs[bank][:].rearrange("p (h d) -> p h d", d=HEAD)
+            pairs = heads[:, :, NOPE:].rearrange("p h (i e) -> p h i e", e=2)
+            cos_part = work.tile([P, HEADS_PER_BANK, ROPE], F32)
+            nc.vector.tensor_mul(
+                out=cos_part[:],
+                in0=heads[:, :, NOPE:],
+                in1=cos_twice[:]
+                .rearrange("p i e -> p (i e)")
+                .unsqueeze(1)
+                .to_broadcast([P, HEADS_PER_BANK, ROPE]),
+            )
+            sin_part = work.tile([P, HEADS_PER_BANK, 2, PAIRS], F32)
+            nc.vector.tensor_mul(
+                out=sin_part[:, :, 0, :],
+                in0=pairs[:, :, :, 1],
+                in1=sin_minus[:].unsqueeze(1).to_broadcast([P, HEADS_PER_BANK, PAIRS]),
+            )
+            nc.vector.tensor_mul(
+                out=sin_part[:, :, 1, :],
+                in0=pairs[:, :, :, 0],
+                in1=sin_plus[:].unsqueeze(1).to_broadcast([P, HEADS_PER_BANK, PAIRS]),
+            )
+            nc.scalar.copy(out=result[:, bank, :, :NOPE], in_=heads[:, :, :NOPE])
+            nc.vector.tensor_add(
+                out=result[:, bank, :, NOPE:].rearrange("p h (i e) -> p h i e", e=2),
+                in0=cos_part[:].rearrange("p h (i e) -> p h i e", e=2),
+                in1=sin_part[:].rearrange("p h e i -> p h i e"),
+            )
+
+        for bank in range(BANKS):
+            nc.sync.dma_start(
+                out=out_rows[:, bank * BANK : (bank + 1) * BANK],
+                in_=result[:, bank].rearrange("p h d -> p (h d)"),
+            )

@@ -30,6 +30,7 @@ BODY_GROUPS = GROUPS - FINISH_GROUPS
 SCALE_GROUPS_PER_DMA = 2
 QUANT_GROUPS = 4
 W_BUFS = 8
+AHEAD_GROUPS = W_BUFS
 PIECE_BUFS = 4
 
 FLOPS = 2 * P * K * N
@@ -61,6 +62,13 @@ def tile_multiheadlatentattention_pb_k_kernel(tc, x, freq_cis, Wq_words, Wq_scal
         w_planes = keep.tile([P, GROUPS, N], U8, align_bytes=64)
         for g0 in range(0, GROUPS, SCALE_GROUPS_PER_DMA):
             nc.vector.memset(w_planes[:, g0 : g0 + SCALE_GROUPS_PER_DMA, :].bitcast(I32), 0)
+
+        def load_group(g):
+            w_group = w_pool.tile([P, 2 * N], U8, align_bytes=64)
+            nc.sync.dma_start(out=w_group[:].bitcast(I32), in_=w_words_dram[g])
+            return w_group
+
+        w_groups = [load_group(g) for g in range(AHEAD_GROUPS)]
 
         for g0 in range(0, GROUPS, SCALE_GROUPS_PER_DMA):
             g_sel = slice(g0, g0 + SCALE_GROUPS_PER_DMA)
@@ -121,10 +129,10 @@ def tile_multiheadlatentattention_pb_k_kernel(tc, x, freq_cis, Wq_words, Wq_scal
 
         accs = [psum.tile([P, BANK], F32, tag="bank", name="acc%d" % bank) for bank in range(BANKS)]
         for g in range(BODY_GROUPS):
-            w_group = w_pool.tile([P, 2 * N], U8, align_bytes=64)
-            nc.sync.dma_start(out=w_group[:].bitcast(I32), in_=w_words_dram[g])
+            if g >= AHEAD_GROUPS:
+                w_groups.append(load_group(g))
             for bank in range(BANKS):
-                one_pass(accs[bank], g, bank, w_group[:, bank * 2 * BANK : (bank + 1) * 2 * BANK])
+                one_pass(accs[bank], g, bank, w_groups[g][:, bank * 2 * BANK : (bank + 1) * 2 * BANK])
 
         result = keep.tile([P, BANKS, HEADS_PER_BANK, HEAD], F32)
         for bank in range(BANKS):

@@ -59,9 +59,12 @@ def tile_multiheadlatentattention_pb_k_kernel(tc, x, freq_cis, Wq_words, Wq_scal
         identity = keep.tile([P, P], F32)
         make_identity(nc, identity[:])
 
-        w_planes = keep.tile([P, GROUPS, N], U8, align_bytes=64)
-        for g0 in range(0, GROUPS, SCALE_GROUPS_PER_DMA):
-            nc.vector.memset(w_planes[:, g0 : g0 + SCALE_GROUPS_PER_DMA, :].bitcast(I32), 0)
+        w_planes = [
+            keep.tile([P, SCALE_GROUPS_PER_DMA, N], U8, align_bytes=64, name="w_planes%d" % j)
+            for j in range(GROUPS // SCALE_GROUPS_PER_DMA)
+        ]
+        for planes in w_planes:
+            nc.vector.memset(planes[:].bitcast(I32), 0)
 
         def load_group(g):
             w_group = w_pool.tile([P, 2 * N], U8, align_bytes=64)
@@ -70,12 +73,12 @@ def tile_multiheadlatentattention_pb_k_kernel(tc, x, freq_cis, Wq_words, Wq_scal
 
         w_groups = [load_group(g) for g in range(AHEAD_GROUPS)]
 
-        for g0 in range(0, GROUPS, SCALE_GROUPS_PER_DMA):
-            g_sel = slice(g0, g0 + SCALE_GROUPS_PER_DMA)
+        for j, planes in enumerate(w_planes):
+            g_sel = slice(j * SCALE_GROUPS_PER_DMA, (j + 1) * SCALE_GROUPS_PER_DMA)
             for q in range(8):
                 partition = 32 * (q // 4) + q % 4
                 nc.sync.dma_start(
-                    out=w_planes[partition:P:64, g_sel, :].bitcast(I32),
+                    out=planes[partition:P:64, :, :].bitcast(I32),
                     in_=w_scales_dram[g_sel, q:16:8, :].rearrange("g j n -> j g n"),
                 )
 
@@ -122,7 +125,9 @@ def tile_multiheadlatentattention_pb_k_kernel(tc, x, freq_cis, Wq_words, Wq_scal
                 lhsT=x_codes[:, g, :].bitcast(FP8X4),
                 lhsT_scale=x_planes[:, g, :],
                 rhs=w_codes.bitcast(FP4X4),
-                rhs_scale=w_planes[:, g, bank * BANK : (bank + 1) * BANK],
+                rhs_scale=w_planes[g // SCALE_GROUPS_PER_DMA][
+                    :, g % SCALE_GROUPS_PER_DMA, bank * BANK : (bank + 1) * BANK
+                ],
                 start=(g == 0),
                 stop=(g == GROUPS - 1),
             )

@@ -27,7 +27,7 @@ HEADS_PER_BANK = BANK // HEAD
 FINISH_GROUPS = 4
 BODY_GROUPS = GROUPS - FINISH_GROUPS
 
-SCALE_GROUPS_PER_DMA = 2
+SCALE_RUN = [2, 4, 4, 4, 2]
 QUANT_GROUPS = 4
 W_BUFS = 8
 AHEAD_GROUPS = W_BUFS
@@ -60,11 +60,12 @@ def tile_multiheadlatentattention_pb_k_kernel(tc, x, freq_cis, Wq_words, Wq_scal
         make_identity(nc, identity[:])
 
         w_planes = [
-            keep.tile([P, SCALE_GROUPS_PER_DMA, N], U8, align_bytes=64, name="w_planes%d" % j)
-            for j in range(GROUPS // SCALE_GROUPS_PER_DMA)
+            keep.tile([P, groups, N], U8, align_bytes=64, name="w_planes%d" % j)
+            for j, groups in enumerate(SCALE_RUN)
         ]
         for planes in w_planes:
             nc.vector.memset(planes[:].bitcast(I32), 0)
+        plane_of_group = [planes[:, i, :] for planes, groups in zip(w_planes, SCALE_RUN) for i in range(groups)]
 
         def load_group(g):
             w_group = w_pool.tile([P, 2 * N], U8, align_bytes=64)
@@ -74,7 +75,7 @@ def tile_multiheadlatentattention_pb_k_kernel(tc, x, freq_cis, Wq_words, Wq_scal
         w_groups = [load_group(g) for g in range(AHEAD_GROUPS)]
 
         for j, planes in enumerate(w_planes):
-            g_sel = slice(j * SCALE_GROUPS_PER_DMA, (j + 1) * SCALE_GROUPS_PER_DMA)
+            g_sel = slice(sum(SCALE_RUN[:j]), sum(SCALE_RUN[: j + 1]))
             for q in range(8):
                 partition = 32 * (q // 4) + q % 4
                 nc.sync.dma_start(
@@ -125,9 +126,7 @@ def tile_multiheadlatentattention_pb_k_kernel(tc, x, freq_cis, Wq_words, Wq_scal
                 lhsT=x_codes[:, g, :].bitcast(FP8X4),
                 lhsT_scale=x_planes[:, g, :],
                 rhs=w_codes.bitcast(FP4X4),
-                rhs_scale=w_planes[g // SCALE_GROUPS_PER_DMA][
-                    :, g % SCALE_GROUPS_PER_DMA, bank * BANK : (bank + 1) * BANK
-                ],
+                rhs_scale=plane_of_group[g][:, bank * BANK : (bank + 1) * BANK],
                 start=(g == 0),
                 stop=(g == GROUPS - 1),
             )

@@ -31,6 +31,8 @@ SCALE_RUN = [2, 4, 4, 4, 2]
 QUANT_GROUPS = 4
 W_BUFS = 8
 AHEAD_GROUPS = W_BUFS
+WARM_GROUP = AHEAD_GROUPS - 2
+WARM_MATMULS = 12
 PIECE_BUFS = 4
 
 FLOPS = 2 * P * K * N
@@ -119,6 +121,14 @@ def tile_multiheadlatentattention_pb_k_kernel(tc, x, freq_cis, Wq_words, Wq_scal
                 scales=x_planes[:, g_sel, :].rearrange("p g n -> p (g n)"),
                 in_=grouped[:, g_sel].rearrange("p g n t -> p (g n t)"),
             )
+
+        landed = keep.tile([P, 16], I32)
+        nc.vector.tensor_copy(out=landed[:], in_=w_groups[WARM_GROUP][:, :64].bitcast(I32))
+        zeros = keep.tile([P, BANK], BF16)
+        nc.vector.memset(zeros[:], 0.0)
+        warm = psum.tile([P, BANK], F32, tag="bank")
+        for i in range(WARM_MATMULS):
+            nc.tensor.matmul(warm[:], lhsT=zeros[:, :P], rhs=zeros[:], start=True, stop=True)
 
         def one_pass(acc, g, bank, w_codes):
             nc.tensor.matmul_mx(

from contextlib import ExitStack

import concourse.mybir as mybir
from concourse.masks import make_identity

BF16 = mybir.dt.bfloat16
F32 = mybir.dt.float32
I32 = mybir.dt.int32
U8 = mybir.dt.uint8
U32 = mybir.dt.uint32
FP8X4 = mybir.dt.float8_e4m3fn_x4
FP4X4 = mybir.dt.float4_e2m1fn_x4

P = 128
K = 8192
N = 4096
K_GROUP = 512
GROUPS = K // K_GROUP
BANK = 512
BANKS = N // BANK
HEAD = 256
NOPE = 128
ROPE = 128
PAIRS = ROPE // 2
HEADS_PER_BANK = BANK // HEAD

FINISH_GROUPS = 4
BODY_GROUPS = GROUPS - FINISH_GROUPS

SCALE_RUN = [2, 4, 4, 4, 2]
QUANT_GROUPS = 4
W_BUFS = 8
AHEAD_GROUPS = W_BUFS
WARM_GROUP = AHEAD_GROUPS - 2
WARM_MATMULS = 12
PIECE_BUFS = 4

FLOPS = 2 * P * K * N


def tile_multiheadlatentattention_pb_k_kernel(tc, x, freq_cis, Wq_words, Wq_scales, out):
    nc = tc.nc
    x_rows = x.rearrange("b t k -> (b t) k")
    out_rows = out.rearrange("b t h d -> (b t) (h d)")
    w_words_dram = Wq_words.bitcast(I32)
    w_scales_dram = Wq_scales.bitcast(I32)

    with ExitStack() as ctx:
        keep = ctx.enter_context(tc.tile_pool(name="keep", bufs=1))
        w_pool = ctx.enter_context(tc.tile_pool(name="w_pool", bufs=W_BUFS))
        piece_pool = ctx.enter_context(tc.tile_pool(name="piece_pool", bufs=PIECE_BUFS))
        work = ctx.enter_context(tc.tile_pool(name="work", bufs=2))
        psum = ctx.enter_context(tc.psum_pool(name="psum", bufs=BANKS))
        ctx.enter_context(tc.manual_schedule())

        x_sb = keep.tile([P, K], BF16, align_bytes=64)
        nc.sync.dma_start(out=x_sb[:], in_=x_rows)
        angles = keep.tile([P, PAIRS, 2], BF16)
        nc.scalar.dma_start(out=angles[:], in_=freq_cis)

        identity = keep.tile([P, P], F32)
        make_identity(nc, identity[:])

        w_planes = [
            keep.tile([P, groups, N], U8, align_bytes=64, name="w_planes%d" % j)
            for j, groups in enumerate(SCALE_RUN)
        ]
        for planes in w_planes:
            nc.vector.memset(planes[:].bitcast(I32), 0)
        plane_of_group = [planes[:, i, :] for planes, groups in zip(w_planes, SCALE_RUN) for i in range(groups)]

        def load_group(g):
            w_group = w_pool.tile([P, 2 * N], U8, align_bytes=64)
            nc.sync.dma_start(out=w_group[:].bitcast(I32), in_=w_words_dram[g])
            return w_group

        w_groups = [load_group(g) for g in range(AHEAD_GROUPS)]

        for j, planes in enumerate(w_planes):
            g_sel = slice(sum(SCALE_RUN[:j]), sum(SCALE_RUN[: j + 1]))
            for q in range(8):
                partition = 32 * (q // 4) + q % 4
                nc.sync.dma_start(
                    out=planes[partition:P:64, :, :].bitcast(I32),
                    in_=w_scales_dram[g_sel, q:16:8, :].rearrange("g j n -> j g n"),
                )

        x_pairs = x_sb[:].bitcast(F32)
        grouped = keep.tile([P, GROUPS, P, 4], BF16, align_bytes=64)
        x_codes = keep.tile([P, GROUPS, P], U32, align_bytes=64)
        x_planes = keep.tile([P, GROUPS, P], U8, align_bytes=64)
        for g0 in range(0, GROUPS, 2):
            flipped = psum.tile([P, 2, 2, P], F32, tag="bank")
            for i in range(2):
                first = (K_GROUP // 2) * (g0 + i)
                for u in range(2):
                    nc.tensor.transpose(
                        flipped[:, i, u, :],
                        x_pairs[:, first + u : first + K_GROUP // 2 : 2],
                        identity[:],
                    )
            nc.scalar.copy(
                out=grouped[:, g0 : g0 + 2]
                .rearrange("p g n t -> p g (n t)")
                .bitcast(F32)
                .rearrange("p g (n u) -> p g n u", u=2),
                in_=flipped[:].rearrange("p g u n -> p g n u"),
            )

        cos_twice = keep.tile([P, PAIRS, 2], F32)
        nc.vector.tensor_copy(out=cos_twice[:], in_=angles[:, :, 0:1].to_broadcast([P, PAIRS, 2]))
        sin_plus = keep.tile([P, PAIRS], F32)
        nc.vector.tensor_copy(out=sin_plus[:], in_=angles[:, :, 1])
        sin_minus = keep.tile([P, PAIRS], F32)
        nc.vector.tensor_scalar_mul(out=sin_minus[:], in0=angles[:, :, 1], scalar1=-1.0)

        for g0 in range(0, GROUPS, QUANT_GROUPS):
            g_sel = slice(g0, g0 + QUANT_GROUPS)
            nc.vector.quantize_mx(
                out=x_codes[:, g_sel, :].rearrange("p g n -> p (g n)").bitcast(FP8X4),
                scales=x_planes[:, g_sel, :].rearrange("p g n -> p (g n)"),
                in_=grouped[:, g_sel].rearrange("p g n t -> p (g n t)"),
            )

        landed = keep.tile([P, 16], I32)
        nc.vector.tensor_copy(out=landed[:], in_=w_groups[WARM_GROUP][:, :64].bitcast(I32))
        zeros = keep.tile([P, BANK], BF16)
        nc.vector.memset(zeros[:], 0.0)
        warm = psum.tile([P, BANK], F32, tag="bank")
        for i in range(WARM_MATMULS):
            nc.tensor.matmul(warm[:], lhsT=zeros[:, :P], rhs=zeros[:], start=True, stop=True)

        def one_pass(acc, g, bank, w_codes):
            nc.tensor.matmul_mx(
                out=acc[:],
                lhsT=x_codes[:, g, :].bitcast(FP8X4),
                lhsT_scale=x_planes[:, g, :],
                rhs=w_codes.bitcast(FP4X4),
                rhs_scale=plane_of_group[g][:, bank * BANK : (bank + 1) * BANK],
                start=(g == 0),
                stop=(g == GROUPS - 1),
            )

        accs = [psum.tile([P, BANK], F32, tag="bank", name="acc%d" % bank) for bank in range(BANKS)]
        for g in range(BODY_GROUPS):
            if g >= AHEAD_GROUPS:
                w_groups.append(load_group(g))
            for bank in range(BANKS):
                one_pass(accs[bank], g, bank, w_groups[g][:, bank * 2 * BANK : (bank + 1) * 2 * BANK])

        result = keep.tile([P, BANKS, HEADS_PER_BANK, HEAD], F32)
        for bank in range(BANKS):
            piece = piece_pool.tile([P, FINISH_GROUPS, 2 * BANK], U8, align_bytes=64)
            nc.sync.dma_start(
                out=piece[:].bitcast(I32),
                in_=w_words_dram[BODY_GROUPS:GROUPS, :, bank * BANK // 2 : (bank + 1) * BANK // 2].rearrange(
                    "g p n -> p g n"
                ),
            )
            for i in range(FINISH_GROUPS):
                one_pass(accs[bank], BODY_GROUPS + i, bank, piece[:, i, :])

            heads = accs[bank][:].rearrange("p (h d) -> p h d", d=HEAD)
            pairs = heads[:, :, NOPE:].rearrange("p h (i e) -> p h i e", e=2)
            cos_part = work.tile([P, HEADS_PER_BANK, ROPE], F32)
            nc.vector.tensor_mul(
                out=cos_part[:],
                in0=heads[:, :, NOPE:],
                in1=cos_twice[:]
                .rearrange("p i e -> p (i e)")
                .unsqueeze(1)
                .to_broadcast([P, HEADS_PER_BANK, ROPE]),
            )
            sin_part = work.tile([P, HEADS_PER_BANK, 2, PAIRS], F32)
            nc.vector.tensor_mul(
                out=sin_part[:, :, 0, :],
                in0=pairs[:, :, :, 1],
                in1=sin_minus[:].unsqueeze(1).to_broadcast([P, HEADS_PER_BANK, PAIRS]),
            )
            nc.vector.tensor_mul(
                out=sin_part[:, :, 1, :],
                in0=pairs[:, :, :, 0],
                in1=sin_plus[:].unsqueeze(1).to_broadcast([P, HEADS_PER_BANK, PAIRS]),
            )
            nc.scalar.copy(out=result[:, bank, :, :NOPE], in_=heads[:, :, :NOPE])
            nc.vector.tensor_add(
                out=result[:, bank, :, NOPE:].rearrange("p h (i e) -> p h i e", e=2),
                in0=cos_part[:].rearrange("p h (i e) -> p h i e", e=2),
                in1=sin_part[:].rearrange("p h e i -> p h i e"),
            )

        for bank in range(BANKS):
            nc.sync.dma_start(
                out=out_rows[:, bank * BANK : (bank + 1) * BANK],
                in_=result[:, bank].rearrange("p h d -> p (h d)"),
            )
